import numpy as np
import ml_dtypes


def mxq(x, axis, fmt="e4m3"):
    dtype, down = {"e4m3": (ml_dtypes.float8_e4m3fn, 7), "e5m2": (ml_dtypes.float8_e5m2, 14)}[fmt]
    v = np.moveaxis(np.asarray(x, np.float32).astype(ml_dtypes.bfloat16).astype(np.float64), axis, -1)
    blocks = v.reshape(v.shape[:-1] + (-1, 32))
    amax = np.abs(blocks).max(-1, keepdims=True)
    byte = np.maximum(np.where(amax > 0, np.frexp(amax)[1] - 1 + 127, 0) - down, 1)
    scale = np.exp2(byte - 127.0)
    codes = (blocks / scale).astype(np.float32).astype(dtype).astype(np.float64)
    return np.moveaxis((codes * scale).reshape(v.shape), -1, axis)


WIDE = False


def mx_kscale(k):
    if not WIDE:
        return np.ones(k)
    levels = np.array([10, -10, 5, -5, 0])
    if k % 512:
        return np.exp2(np.random.permutation(np.resize(levels, k // 32))).repeat(32)
    a = np.empty((k // 512, 16))
    for p in range(k // 512):
        a[p, :8] = np.random.permutation(np.resize(levels, 8))
        for g in range(8):
            far = levels[np.abs(levels - a[p, g]) >= 10]
            a[p, g + 8] = far[np.random.randint(len(far))]
    return np.exp2(a.ravel()).repeat(32)


BF16 = ml_dtypes.bfloat16


def bf(x):
    return np.asarray(x, np.float32).astype(BF16)


def f64(x):
    return np.asarray(x).astype(np.float64)


SL, BS, DM, H, NH, DO = 32, 512, 2048, 32, 64, 2048
DP = H * NH


def setup_inputs():
    s, t = mx_kscale(DM), mx_kscale(DP)
    g = np.random.standard_normal((SL, BS, H)) * 2.0
    return {"values": bf(np.random.standard_normal((SL, BS, DM)) * s),
            "logw": bf(g - np.log(np.exp(g).sum(0, keepdims=True))),
            "Wv": bf(np.random.standard_normal((DP, DM)) / np.sqrt(DM * SL) / s * t[:, None]),
            "Wo": bf(np.random.standard_normal((DO, DP)) * 0.5 / np.sqrt(DP) / t)}


def reference(values, logw, Wv, Wo):
    vp = mxq(f64(values), 2, "e4m3") @ mxq(f64(Wv), 1, "e4m3").T
    attn = (f64(logw)[..., None] * vp.reshape(SL, BS, H, NH)).sum(0)
    return mxq(attn.reshape(BS, DP), 1, "e4m3") @ mxq(f64(Wo), 1, "e4m3").T

@@ -1,0 +1,205 @@
+from contextlib import ExitStack
+
+import concourse.mybir as mybir
+from concourse.masks import make_identity
+
+SL, BS, DM, H, NH, DO = 32, 512, 2048, 32, 64, 2048
+DP = H * NH
+FLOPS = 2 * SL * BS * DM * DP + 2 * BS * DP * DO
+
+F32 = mybir.dt.float32
+BF16 = mybir.dt.bfloat16
+U32 = mybir.dt.uint32
+U8 = mybir.dt.uint8
+FP8X4 = mybir.dt.float8_e4m3fn_x4
+ALU = mybir.AluOpType
+
+P = 128
+NB = BS // P
+HEAD_ORDER = (0, 2, 4, 6, 1, 3, 5, 7)
+
+
+def tile_multiheadattention_pb_l_kernel(tc, values, logw, Wv, Wo, out):
+    nc = tc.nc
+    with ExitStack() as ctx:
+        keep = ctx.enter_context(tc.tile_pool(name="keep", bufs=1))
+        stream = ctx.enter_context(tc.tile_pool(name="stream", bufs=2))
+        psum = ctx.enter_context(tc.psum_pool(name="psum", bufs=2))
+        ctx.enter_context(tc.manual_schedule())
+
+        ident = keep.tile([P, P], F32, name="ident")
+        make_identity(nc, ident[:])
+        wv_codes = keep.tile([P, 4, DP], U32, name="wv_codes", align_bytes=64)
+        wv_scales = keep.tile([P, 4, DP], U8, name="wv_scales", align_bytes=64)
+        wo_codes = keep.tile([P, 4, DO], U32, name="wo_codes", align_bytes=64)
+        wo_scales = keep.tile([P, 4, DO], U8, name="wo_scales", align_bytes=64)
+
+        jobs = [("wv", r, 0) for r in range(DP // P)]
+        for bt in range(NB):
+            for s in range(SL):
+                jobs.append(("v", s, bt))
+                if bt == 0 and s % 2 == 1:
+                    jobs.append(("wo", s // 2, 0))
+        nj = len(jobs)
+        last_job = [jobs.index(("v", SL - 1, bt)) for bt in range(NB)]
+
+        raw, srt, trn, grp, cod, scl, bank = {}, {}, {}, {}, {}, {}, {}
+        lw, acc, ga, ac, asc = {}, {}, {}, {}, {}
+
+        def load(j):
+            kind, a, bt = jobs[j]
+            if kind == "wv":
+                rows = Wv[P * a : P * a + P, :]
+            elif kind == "wo":
+                rows = Wo[P * a : P * a + P, :]
+            else:
+                rows = values[a, P * bt : P * bt + P, :]
+            r = stream.tile([P, 4, 512], BF16, name="raw", tag="raw", bufs=4)
+            raw[j] = r
+            for q in range(4):
+                nc.sync.dma_start(
+                    out=r[32 * q : 32 * q + 32, :, :],
+                    in_=rows[:, 512 * q : 512 * q + 512].rearrange("(tg b) k -> b tg k", b=32),
+                )
+            if kind == "v" and a == 0:
+                lwr = stream.tile([P, SL, H], BF16, name="lwr", tag="lwr", bufs=2)
+                nc.sync.dma_start(out=lwr[:], in_=logw[:, P * bt : P * bt + P, :].rearrange("s b h -> b s h"))
+                lwf = stream.tile([P, SL * H], F32, name="lwf", tag="lwf", bufs=2)
+                lw[bt] = lwf
+                nc.gpsimd.tensor_copy(out=lwf[:], in_=lwr[:].rearrange("p s h -> p (s h)"))
+
+        def sort(j):
+            words = raw[j][:].bitcast(F32)
+            sd = stream.tile([P, 1024], F32, name="srt", tag="srt", bufs=2, align_bytes=64)
+            srt[j] = sd
+            view = sd[:].rearrange("p (g tg u x) -> p g tg u x", g=4, tg=4, u=2)
+            for g in range(4):
+                nc.scalar.copy(
+                    out=view[:, g],
+                    in_=words[:, :, 64 * g : 64 * g + 64].rearrange("p tg (x u) -> p tg u x", u=2),
+                )
+
+        def turn(j):
+            t = stream.tile([P, 1024], F32, name="trn", tag="trn", bufs=2, align_bytes=64)
+            trn[j] = t
+            nc.vector.transpose(out=t[:], in_=srt[j][:])
+
+        def interleave(j):
+            gd = stream.tile([P, 2048], BF16, name="grp", tag="grp", bufs=2, align_bytes=64)
+            grp[j] = gd
+            nc.scalar.copy(
+                out=gd[:].bitcast(F32).rearrange("p (c b u) -> p c b u", c=16, u=2),
+                in_=trn[j][:].rearrange("p (c u b) -> p c b u", c=16, u=2),
+            )
+
+        def quantise(j):
+            kind, a, bt = jobs[j]
+            gd = grp[j]
+            if kind == "v":
+                c = stream.tile([P, 512], U32, name="cod", tag="cod", bufs=3, align_bytes=64)
+                sc = stream.tile([P, 512], U8, name="scl", tag="scl", bufs=3, align_bytes=64)
+                cod[j] = c
+                scl[j] = sc
+                nc.vector.quantize_mx(out=c[:].bitcast(FP8X4), scales=sc[:], in_=gd[:])
+            else:
+                codes = wv_codes if kind == "wv" else wo_codes
+                scales = wv_scales if kind == "wv" else wo_scales
+                for g in range(4):
+                    nc.vector.quantize_mx(
+                        out=codes[:, g, P * a : P * a + P].bitcast(FP8X4),
+                        scales=scales[:, g, P * a : P * a + P],
+                        in_=gd[:, 512 * g : 512 * g + 512],
+                    )
+
+        def mx_group(c, sc, w_codes, w_scales, n):
+            ps = psum.tile([P, 512], F32, name="mm", tag="mm", bufs=6)
+            for g in range(4):
+                nc.tensor.matmul_mx(
+                    out=ps[:],
+                    lhsT=c[:, P * g : P * g + P].bitcast(FP8X4),
+                    lhsT_scale=sc[:, P * g : P * g + P],
+                    rhs=w_codes[:, g, 512 * n : 512 * n + 512].bitcast(FP8X4),
+                    rhs_scale=w_scales[:, g, 512 * n : 512 * n + 512],
+                    start=(g == 0),
+                    stop=(g == 3),
+                )
+            return ps
+
+        def pool_bank(j, n):
+            kind, s, bt = jobs[j]
+            ps = bank[(j, n)]
+            if s == 0 and n == 0:
+                a_new = stream.tile([P, 4, 4, P], F32, name="acc", tag="acc", bufs=2)
+                acc[bt] = a_new
+            a = acc[bt]
+            for hh in HEAD_ORDER:
+                src = ps[:, 64 * hh : 64 * hh + 64].rearrange("p (x t) -> p t x", t=4)
+                lo = 32 * n + 16 * (hh % 2)
+                dst = a[:, hh // 2, :, lo : lo + 16]
+                col = H * s + 8 * n + hh
+                w = lw[bt][:, col : col + 1]
+                if s == 0:
+                    nc.vector.tensor_scalar(out=dst, in0=src, scalar1=w, scalar2=None, op0=ALU.mult)
+                else:
+                    nc.vector.scalar_tensor_tensor(out=dst, in0=src, scalar=w, in1=dst, op0=ALU.mult, op1=ALU.add)
+
+        def s2_turn(bt, gs):
+            if bt not in ga:
+                g_new = stream.tile([P, 2048], BF16, name="ga", tag="ga", bufs=2, align_bytes=64)
+                ga[bt] = g_new
+            view = ga[bt][:].rearrange("p (g b t) -> p g b t", g=4, t=4)
+            for g in gs:
+                tp = psum.tile([P, 4, P], F32, name="tp", tag="tp", bufs=2)
+                for t in range(4):
+                    nc.tensor.transpose(tp[:, t, :], acc[bt][:, g, t, :], ident[:])
+                nc.scalar.copy(out=view[:, g], in_=tp[:].rearrange("p t b -> p b t"))
+
+        def s2_quantise(bt):
+            c = stream.tile([P, 512], U32, name="ac", tag="ac", bufs=2, align_bytes=64)
+            sc = stream.tile([P, 512], U8, name="asc", tag="asc", bufs=2, align_bytes=64)
+            ac[bt] = c
+            asc[bt] = sc
+            nc.vector.quantize_mx(out=c[:].bitcast(FP8X4), scales=sc[:], in_=ga[bt][:])
+
+        def s2_multiply(bt, n):
+            ps = mx_group(ac[bt], asc[bt], wo_codes, wo_scales, n)
+            ob = stream.tile([P, 512], F32, name="ob", tag="ob", bufs=4)
+            nc.scalar.copy(out=ob[:], in_=ps[:])
+            nc.gpsimd.dma_start(out=out[P * bt : P * bt + P, 512 * n : 512 * n + 512], in_=ob[:])
+
+        pending = []
+        done = 0
+        for step in range(-6, nj + 9):
+            for bt in range(NB):
+                late = step - last_job[bt]
+                if late == 2:
+                    s2_turn(bt, (0, 1))
+                if late == 3:
+                    s2_turn(bt, (2, 3))
+                if late == 4:
+                    s2_quantise(bt)
+                if 5 <= late < 9:
+                    s2_multiply(bt, late - 5)
+            if 0 <= step + 6 < nj:
+                load(step + 6)
+            if 0 <= step + 2 < nj:
+                interleave(step + 2)
+            if 0 <= step + 4 < nj:
+                sort(step + 4)
+            if 0 <= step + 1 < nj:
+                quantise(step + 1)
+            if done < len(pending):
+                pool_bank(pending[done][0], pending[done][1])
+                done += 1
+            if 0 <= step + 3 < nj:
+                turn(step + 3)
+            while done < len(pending):
+                pool_bank(pending[done][0], pending[done][1])
+                done += 1
+            if 0 <= step < nj and jobs[step][0] == "v":
+                for n in range(4):
+                    bank[(step, n)] = mx_group(cod[step], scl[step], wv_codes, wv_scales, n)
+                    pending.append((step, n))
+            while len(pending) - done > 2:
+                pool_bank(pending[done][0], pending[done][1])
+                done += 1

@@ -13,10 +13,13 @@ U32 = mybir.dt.uint32
 U8 = mybir.dt.uint8
 FP8X4 = mybir.dt.float8_e4m3fn_x4
 ALU = mybir.AluOpType
+ACT = mybir.ActivationFunctionType
 
 P = 128
 NB = BS // P
-HEAD_ORDER = (0, 2, 4, 6, 1, 3, 5, 7)
+NW = DP // P
+WO_EVERY = 6
+POOL_BY = ("scalar", "vector", "wide", "vector")
 
 
 def tile_multiheadattention_pb_l_kernel(tc, values, logw, Wv, Wo, out):
@@ -29,31 +32,65 @@ def tile_multiheadattention_pb_l_kernel(tc, values, logw, Wv, Wo, out):
 
         ident = keep.tile([P, P], F32, name="ident")
         make_identity(nc, ident[:])
+        warm = keep.tile([P, 8], F32, name="warm")
+        nc.scalar.activation(out=warm[:, 0:1], in_=ident[:, 0:1], func=ACT.Copy, scale=1.0)
         wv_codes = keep.tile([P, 4, DP], U32, name="wv_codes", align_bytes=64)
         wv_scales = keep.tile([P, 4, DP], U8, name="wv_scales", align_bytes=64)
         wo_codes = keep.tile([P, 4, DO], U32, name="wo_codes", align_bytes=64)
         wo_scales = keep.tile([P, 4, DO], U8, name="wo_scales", align_bytes=64)
 
-        jobs = [("wv", r, 0) for r in range(DP // P)]
+        jobs = []
         for bt in range(NB):
             for s in range(SL):
                 jobs.append(("v", s, bt))
-                if bt == 0 and s % 2 == 1:
-                    jobs.append(("wo", s // 2, 0))
+                seen = bt * SL + s + 1
+                if seen % WO_EVERY == 0 and seen // WO_EVERY <= NW:
+                    jobs.append(("wo", seen // WO_EVERY - 1, 0))
         nj = len(jobs)
         last_job = [jobs.index(("v", SL - 1, bt)) for bt in range(NB)]
+        s2_first = jobs.index(("wo", NW - 1, 0)) + 2
 
         raw, srt, trn, grp, cod, scl, bank = {}, {}, {}, {}, {}, {}, {}
         lw, acc, ga, ac, asc = {}, {}, {}, {}, {}
+        hraw, hsrt, hps, hgrp = {}, {}, {}, {}
+
+        def head_load(r):
+            t = stream.tile([P, 4, 512], BF16, name="hraw", tag="hraw", bufs=4)
+            hraw[r] = t
+            nc.sync.dma_start(out=t[:].rearrange("p q k -> p (q k)"), in_=Wv[P * r : P * r + P, :])
+
+        def head_permute(r):
+            t = stream.tile([P, 1024], F32, name="hsrt", tag="hsrt", bufs=2)
+            hsrt[r] = t
+            nc.vector.tensor_copy(
+                out=t[:].rearrange("p (g q w) -> p g q w", g=4, q=4),
+                in_=hraw[r][:].bitcast(F32).rearrange("p q (g w) -> p g q w", g=4),
+            )
+
+        def head_turn(r):
+            gd = stream.tile([P, 2048], BF16, name="hgrp", tag="hgrp", bufs=2, align_bytes=64)
+            hgrp[r] = gd
+            for half in range(2):
+                pt = psum.tile([P, 512], F32, name="mm", tag="mm", bufs=6)
+                for j in range(4):
+                    lo = 256 * (2 * half + j // 2) + j % 2
+                    nc.tensor.transpose(pt[:, P * j : P * j + P], hsrt[r][:, lo : lo + 255 : 2], ident[:])
+                nc.scalar.copy(
+                    out=gd[:].bitcast(F32)[:, 512 * half : 512 * half + 512].rearrange("p (g c u) -> p g c u", g=2, u=2),
+                    in_=pt[:].rearrange("p (g u c) -> p g c u", g=2, u=2),
+                )
+
+        def quantise_weight(gd, codes, scales, block):
+            for g in range(4):
+                nc.vector.quantize_mx(
+                    out=codes[:, g, P * block : P * block + P].bitcast(FP8X4),
+                    scales=scales[:, g, P * block : P * block + P],
+                    in_=gd[:, 512 * g : 512 * g + 512],
+                )
 
         def load(j):
             kind, a, bt = jobs[j]
-            if kind == "wv":
-                rows = Wv[P * a : P * a + P, :]
-            elif kind == "wo":
-                rows = Wo[P * a : P * a + P, :]
-            else:
-                rows = values[a, P * bt : P * bt + P, :]
+            rows = Wo[P * a : P * a + P, :] if kind == "wo" else values[a, P * bt : P * bt + P, :]
             r = stream.tile([P, 4, 512], BF16, name="raw", tag="raw", bufs=4)
             raw[j] = r
             for q in range(4):
@@ -64,9 +101,13 @@ def tile_multiheadattention_pb_l_kernel(tc, values, logw, Wv, Wo, out):
             if kind == "v" and a == 0:
                 lwr = stream.tile([P, SL, H], BF16, name="lwr", tag="lwr", bufs=2)
                 nc.sync.dma_start(out=lwr[:], in_=logw[:, P * bt : P * bt + P, :].rearrange("s b h -> b s h"))
-                lwf = stream.tile([P, SL * H], F32, name="lwf", tag="lwf", bufs=2)
+                lwf = stream.tile([P, SL, 4, 8], F32, name="lwf", tag="lwf", bufs=2)
                 lw[bt] = lwf
-                nc.gpsimd.tensor_copy(out=lwf[:], in_=lwr[:].rearrange("p s h -> p (s h)"))
+                for n in range(4):
+                    nc.gpsimd.tensor_copy(
+                        out=lwf[:, :, n, :].rearrange("p s (a c) -> p s a c", a=4),
+                        in_=lwr[:].rearrange("p s (a m c) -> p s a m c", a=4, m=4)[:, :, :, n, :],
+                    )
 
         def sort(j):
             words = raw[j][:].bitcast(F32)
@@ -94,112 +135,158 @@ def tile_multiheadattention_pb_l_kernel(tc, values, logw, Wv, Wo, out):
 
         def quantise(j):
             kind, a, bt = jobs[j]
-            gd = grp[j]
-            if kind == "v":
+            if kind == "wo":
+                quantise_weight(grp[j], wo_codes, wo_scales, a)
+            else:
                 c = stream.tile([P, 512], U32, name="cod", tag="cod", bufs=3, align_bytes=64)
                 sc = stream.tile([P, 512], U8, name="scl", tag="scl", bufs=3, align_bytes=64)
                 cod[j] = c
                 scl[j] = sc
-                nc.vector.quantize_mx(out=c[:].bitcast(FP8X4), scales=sc[:], in_=gd[:])
-            else:
-                codes = wv_codes if kind == "wv" else wo_codes
-                scales = wv_scales if kind == "wv" else wo_scales
-                for g in range(4):
-                    nc.vector.quantize_mx(
-                        out=codes[:, g, P * a : P * a + P].bitcast(FP8X4),
-                        scales=scales[:, g, P * a : P * a + P],
-                        in_=gd[:, 512 * g : 512 * g + 512],
-                    )
+                nc.vector.quantize_mx(out=c[:].bitcast(FP8X4), scales=sc[:], in_=grp[j][:])
+
+        def mx_pass(ps, c, sc, w_codes, w_scales, n, g):
+            nc.tensor.matmul_mx(
+                out=ps[:],
+                lhsT=c[:, P * g : P * g + P].bitcast(FP8X4),
+                lhsT_scale=sc[:, P * g : P * g + P],
+                rhs=w_codes[:, g, 512 * n : 512 * n + 512].bitcast(FP8X4),
+                rhs_scale=w_scales[:, g, 512 * n : 512 * n + 512],
+                start=(g == 0),
+                stop=(g == 3),
+            )
 
         def mx_group(c, sc, w_codes, w_scales, n):
             ps = psum.tile([P, 512], F32, name="mm", tag="mm", bufs=6)
             for g in range(4):
-                nc.tensor.matmul_mx(
-                    out=ps[:],
-                    lhsT=c[:, P * g : P * g + P].bitcast(FP8X4),
-                    lhsT_scale=sc[:, P * g : P * g + P],
-                    rhs=w_codes[:, g, 512 * n : 512 * n + 512].bitcast(FP8X4),
-                    rhs_scale=w_scales[:, g, 512 * n : 512 * n + 512],
-                    start=(g == 0),
-                    stop=(g == 3),
-                )
+                mx_pass(ps, c, sc, w_codes, w_scales, n, g)
             return ps
 
         def pool_bank(j, n):
-            kind, s, bt = jobs[j]
+            s, bt = jobs[j][1], jobs[j][2]
             ps = bank[(j, n)]
-            if s == 0 and n == 0:
-                a_new = stream.tile([P, 4, 4, P], F32, name="acc", tag="acc", bufs=2)
-                acc[bt] = a_new
-            a = acc[bt]
-            for hh in HEAD_ORDER:
-                src = ps[:, 64 * hh : 64 * hh + 64].rearrange("p (x t) -> p t x", t=4)
-                lo = 32 * n + 16 * (hh % 2)
-                dst = a[:, hh // 2, :, lo : lo + 16]
-                col = H * s + 8 * n + hh
-                w = lw[bt][:, col : col + 1]
-                if s == 0:
-                    nc.vector.tensor_scalar(out=dst, in0=src, scalar1=w, scalar2=None, op0=ALU.mult)
-                else:
-                    nc.vector.scalar_tensor_tensor(out=dst, in0=src, scalar=w, in1=dst, op0=ALU.mult, op1=ALU.add)
+            if s == 0:
+                a_new = stream.tile([P, 512], F32, name="acc%d" % n, tag="acc%d" % n, bufs=2)
+                acc[(bt, n)] = a_new
+            a = acc[(bt, n)]
+            w = lw[bt][:, s, n, :]
+            how = POOL_BY[n]
+            if how == "vector":
+                for hh in range(8):
+                    cols = slice(64 * hh, 64 * hh + 64)
+                    if s == 0:
+                        nc.vector.tensor_scalar(out=a[:, cols], in0=ps[:, cols], scalar1=w[:, hh : hh + 1], scalar2=None, op0=ALU.mult)
+                    else:
+                        nc.vector.scalar_tensor_tensor(
+                            out=a[:, cols], in0=ps[:, cols], scalar=w[:, hh : hh + 1], in1=a[:, cols], op0=ALU.mult, op1=ALU.add
+                        )
+                return
+            if s == 0:
+                dst = a
+            else:
+                dst = stream.tile([P, 512], F32, name="tmp", tag="tmp", bufs=4)
+            if how == "scalar":
+                for hh in range(8):
+                    cols = slice(64 * hh, 64 * hh + 64)
+                    nc.scalar.activation(out=dst[:, cols], in_=ps[:, cols], func=ACT.Copy, scale=w[:, hh : hh + 1])
+            else:
+                nc.vector.tensor_tensor(
+                    out=dst[:].rearrange("p (h c) -> p h c", h=8),
+                    in0=ps[:].rearrange("p (h c) -> p h c", h=8),
+                    in1=w.rearrange("p (h o) -> p h o", o=1).to_broadcast([P, 8, 64]),
+                    op=ALU.mult,
+                )
+            if s > 0:
+                nc.gpsimd.tensor_tensor(out=a[:], in0=a[:], in1=dst[:], op=ALU.add)
 
-        def s2_turn(bt, gs):
+        def s2_turn(bt, g):
             if bt not in ga:
                 g_new = stream.tile([P, 2048], BF16, name="ga", tag="ga", bufs=2, align_bytes=64)
                 ga[bt] = g_new
-            view = ga[bt][:].rearrange("p (g b t) -> p g b t", g=4, t=4)
-            for g in gs:
-                tp = psum.tile([P, 4, P], F32, name="tp", tag="tp", bufs=2)
-                for t in range(4):
-                    nc.tensor.transpose(tp[:, t, :], acc[bt][:, g, t, :], ident[:])
-                nc.scalar.copy(out=view[:, g], in_=tp[:].rearrange("p t b -> p b t"))
+                c = stream.tile([P, 512], U32, name="ac", tag="ac", bufs=4, align_bytes=64)
+                sc = stream.tile([P, 512], U8, name="asc", tag="asc", bufs=4, align_bytes=64)
+                ac[bt] = c
+                asc[bt] = sc
+            tp = psum.tile([P, 4, P], F32, name="tp", tag="tp", bufs=2)
+            for t in range(4):
+                nc.tensor.transpose(tp[:, t, :], acc[(bt, g)][:, t : t + 509 : 4], ident[:])
+            nc.scalar.copy(
+                out=ga[bt][:, 512 * g : 512 * g + 512].rearrange("p (b t) -> p b t", t=4),
+                in_=tp[:].rearrange("p t b -> p b t"),
+            )
 
-        def s2_quantise(bt):
-            c = stream.tile([P, 512], U32, name="ac", tag="ac", bufs=2, align_bytes=64)
-            sc = stream.tile([P, 512], U8, name="asc", tag="asc", bufs=2, align_bytes=64)
-            ac[bt] = c
-            asc[bt] = sc
-            nc.vector.quantize_mx(out=c[:].bitcast(FP8X4), scales=sc[:], in_=ga[bt][:])
+        def s2_quantise(bt, g):
+            nc.vector.quantize_mx(
+                out=ac[bt][:, P * g : P * g + P].bitcast(FP8X4),
+                scales=asc[bt][:, P * g : P * g + P],
+                in_=ga[bt][:, 512 * g : 512 * g + 512],
+            )
 
-        def s2_multiply(bt, n):
-            ps = mx_group(ac[bt], asc[bt], wo_codes, wo_scales, n)
+        def s2_store(bt, n, ps, engine, queue):
             ob = stream.tile([P, 512], F32, name="ob", tag="ob", bufs=4)
-            nc.scalar.copy(out=ob[:], in_=ps[:])
-            nc.gpsimd.dma_start(out=out[P * bt : P * bt + P, 512 * n : 512 * n + 512], in_=ob[:])
+            if engine == "scalar":
+                nc.scalar.copy(out=ob[:], in_=ps[:])
+            else:
+                nc.vector.tensor_copy(out=ob[:], in_=ps[:])
+            queue.dma_start(out=out[P * bt : P * bt + P, 512 * n : 512 * n + 512], in_=ob[:])
 
-        pending = []
-        done = 0
-        for step in range(-6, nj + 9):
-            for bt in range(NB):
+        def step_body(step):
+            for bt in range(NB - 1):
                 late = step - last_job[bt]
-                if late == 2:
-                    s2_turn(bt, (0, 1))
-                if late == 3:
-                    s2_turn(bt, (2, 3))
+                if late == 2 or late == 3:
+                    s2_turn(bt, 2 * late - 4)
+                    s2_turn(bt, 2 * late - 3)
                 if late == 4:
-                    s2_quantise(bt)
-                if 5 <= late < 9:
-                    s2_multiply(bt, late - 5)
+                    for g in range(4):
+                        s2_quantise(bt, g)
+            if 0 <= step - s2_first < 4 * (NB - 1):
+                bt, n = divmod(step - s2_first, 4)
+                s2_store(bt, n, mx_group(ac[bt], asc[bt], wo_codes, wo_scales, n), "scalar", nc.gpsimd)
             if 0 <= step + 6 < nj:
                 load(step + 6)
             if 0 <= step + 2 < nj:
                 interleave(step + 2)
-            if 0 <= step + 4 < nj:
-                sort(step + 4)
             if 0 <= step + 1 < nj:
                 quantise(step + 1)
-            if done < len(pending):
-                pool_bank(pending[done][0], pending[done][1])
-                done += 1
+            for j in (step - 2, step - 1):
+                if (j, 3) in bank and (j, 3) not in pooled:
+                    pool_bank(j, 3)
+                    pooled.add((j, 3))
             if 0 <= step + 3 < nj:
                 turn(step + 3)
-            while done < len(pending):
-                pool_bank(pending[done][0], pending[done][1])
-                done += 1
-            if 0 <= step < nj and jobs[step][0] == "v":
-                for n in range(4):
+            live = 0 <= step < nj and jobs[step][0] == "v"
+            if live:
+                bank[(step, 0)] = mx_group(cod[step], scl[step], wv_codes, wv_scales, 0)
+                pool_bank(step, 0)
+            if 0 <= step + 4 < nj:
+                sort(step + 4)
+            if live:
+                for n in (1, 2):
                     bank[(step, n)] = mx_group(cod[step], scl[step], wv_codes, wv_scales, n)
-                    pending.append((step, n))
-            while len(pending) - done > 2:
-                pool_bank(pending[done][0], pending[done][1])
-                done += 1
+                    pool_bank(step, n)
+                bank[(step, 3)] = mx_group(cod[step], scl[step], wv_codes, wv_scales, 3)
+
+        pooled = set()
+        for r in range(-4, NW + 1):
+            if 0 <= r < NW:
+                quantise_weight(hgrp[r], wv_codes, wv_scales, 4 * (r % 4) + r // 4)
+            if 0 <= r + 1 < NW:
+                head_turn(r + 1)
+            if 0 <= r + 2 < NW:
+                head_permute(r + 2)
+            if r + 4 < NW:
+                head_load(r + 4)
+            if 4 <= r < NW and r % 2 == 0:
+                step_body((r - 4) // 2 - 6)
+        for step in range(0, nj + 2):
+            step_body(step)
+
+        bt = NB - 1
+        for g in range(4):
+            s2_turn(bt, g)
+            s2_quantise(bt, g)
+        ends = [psum.tile([P, 512], F32, name="mm", tag="mm", bufs=6) for n in range(4)]
+        for g in range(4):
+            for n in range(4):
+                mx_pass(ends[n], ac[bt], asc[bt], wo_codes, wo_scales, n, g)
+        for n in range(4):
+            s2_store(bt, n, ends[n], "scalar" if n % 2 == 0 else "vector", nc.sync if n % 2 == 0 else nc.gpsimd)

@@ -19,7 +19,8 @@ P = 128
 NB = BS // P
 NW = DP // P
 WO_EVERY = 6
-POOL_BY = ("scalar", "vector", "wide", "vector")
+SORT_ON_SCALAR = 3
+POOL_BY = ("scalar", "vector", "scalar", "vector")
 
 
 def tile_multiheadattention_pb_l_kernel(tc, values, logw, Wv, Wo, out):
@@ -51,11 +52,11 @@ def tile_multiheadattention_pb_l_kernel(tc, values, logw, Wv, Wo, out):
         s2_first = jobs.index(("wo", NW - 1, 0)) + 2
 
         raw, srt, trn, grp, cod, scl, bank = {}, {}, {}, {}, {}, {}, {}
-        lw, acc, ga, ac, asc = {}, {}, {}, {}, {}
+        lw, lwb, acc, ga, ac, asc = {}, {}, {}, {}, {}, {}
         hraw, hsrt, hps, hgrp = {}, {}, {}, {}
 
         def head_load(r):
-            t = stream.tile([P, 4, 512], BF16, name="hraw", tag="hraw", bufs=4)
+            t = stream.tile([P, 4, 512], BF16, name="hraw", tag="hraw", bufs=5)
             hraw[r] = t
             nc.sync.dma_start(out=t[:].rearrange("p q k -> p (q k)"), in_=Wv[P * r : P * r + P, :])
 
@@ -101,21 +102,28 @@ def tile_multiheadattention_pb_l_kernel(tc, values, logw, Wv, Wo, out):
             if kind == "v" and a == 0:
                 lwr = stream.tile([P, SL, H], BF16, name="lwr", tag="lwr", bufs=2)
                 nc.sync.dma_start(out=lwr[:], in_=logw[:, P * bt : P * bt + P, :].rearrange("s b h -> b s h"))
+                lwb[bt] = lwr
                 lwf = stream.tile([P, SL, 4, 8], F32, name="lwf", tag="lwf", bufs=2)
                 lw[bt] = lwf
-                for n in range(4):
-                    nc.gpsimd.tensor_copy(
-                        out=lwf[:, :, n, :].rearrange("p s (a c) -> p s a c", a=4),
-                        in_=lwr[:].rearrange("p s (a m c) -> p s a m c", a=4, m=4)[:, :, :, n, :],
+
+        def widen_logw(bt):
+            for n in range(4):
+                if POOL_BY[n] == "scalar":
+                    nc.scalar.copy(
+                        out=lw[bt][:, :, n, :].rearrange("p s (a c) -> p s a c", a=4),
+                        in_=lwb[bt][:].rearrange("p s (a m c) -> p s a m c", a=4, m=4)[:, :, :, n, :],
                     )
 
         def sort(j):
+            if jobs[j][0] == "v" and jobs[j][1] == 0:
+                widen_logw(jobs[j][2])
             words = raw[j][:].bitcast(F32)
             sd = stream.tile([P, 1024], F32, name="srt", tag="srt", bufs=2, align_bytes=64)
             srt[j] = sd
             view = sd[:].rearrange("p (g tg u x) -> p g tg u x", g=4, tg=4, u=2)
             for g in range(4):
-                nc.scalar.copy(
+                mover = nc.scalar.copy if g < SORT_ON_SCALAR else nc.vector.tensor_copy
+                mover(
                     out=view[:, g],
                     in_=words[:, :, 64 * g : 64 * g + 64].rearrange("p tg (x u) -> p tg u x", u=2),
                 )
@@ -173,12 +181,12 @@ def tile_multiheadattention_pb_l_kernel(tc, values, logw, Wv, Wo, out):
             if how == "vector":
                 for hh in range(8):
                     cols = slice(64 * hh, 64 * hh + 64)
+                    h = 8 * (hh // 2) + 2 * n + hh % 2
+                    wb = lwb[bt][:, s, h : h + 1]
                     if s == 0:
-                        nc.vector.tensor_scalar(out=a[:, cols], in0=ps[:, cols], scalar1=w[:, hh : hh + 1], scalar2=None, op0=ALU.mult)
+                        nc.vector.tensor_scalar(out=a[:, cols], in0=ps[:, cols], scalar1=wb, scalar2=None, op0=ALU.mult)
                     else:
-                        nc.vector.scalar_tensor_tensor(
-                            out=a[:, cols], in0=ps[:, cols], scalar=w[:, hh : hh + 1], in1=a[:, cols], op0=ALU.mult, op1=ALU.add
-                        )
+                        nc.vector.scalar_tensor_tensor(out=a[:, cols], in0=ps[:, cols], scalar=wb, in1=a[:, cols], op0=ALU.mult, op1=ALU.add)
                 return
             if s == 0:
                 dst = a
@@ -196,7 +204,9 @@ def tile_multiheadattention_pb_l_kernel(tc, values, logw, Wv, Wo, out):
                     op=ALU.mult,
                 )
             if s > 0:
-                nc.gpsimd.tensor_tensor(out=a[:], in0=a[:], in1=dst[:], op=ALU.add)
+                for part in range(2):
+                    cs = slice(256 * part, 256 * part + 256)
+                    nc.gpsimd.tensor_tensor(out=a[:, cs], in0=a[:, cs], in1=dst[:, cs], op=ALU.add)
 
         def s2_turn(bt, g):
             if bt not in ga:
@@ -289,4 +299,4 @@ def tile_multiheadattention_pb_l_kernel(tc, values, logw, Wv, Wo, out):
             for n in range(4):
                 mx_pass(ends[n], ac[bt], asc[bt], wo_codes, wo_scales, n, g)
         for n in range(4):
-            s2_store(bt, n, ends[n], "scalar" if n % 2 == 0 else "vector", nc.sync if n % 2 == 0 else nc.gpsimd)
+            s2_store(bt, n, ends[n], "scalar" if n % 2 == 0 else "vector", nc.sync if n % 2 == 0 else nc.scalar)

@@ -16,11 +16,17 @@ ALU = mybir.AluOpType
 ACT = mybir.ActivationFunctionType
 
 P = 128
-NB = BS // P
-NW = DP // P
+PASSES = 4
+BANK = 512
+BANKS = DP // BANK
+HEADS = BANK // NH
+BATCH_TILES = BS // P
+W_TILES = DP // P
+
 WO_EVERY = 6
-SORT_ON_SCALAR = 3
-POOL_BY = ("scalar", "vector", "scalar", "vector")
+SORTS_ON_SCALAR = 3
+LOAD_AHEAD, SORT_AHEAD, TURN_AHEAD, INTERLEAVE_AHEAD, QUANTISE_AHEAD = 6, 4, 3, 2, 1
+STREAM_STARTS = 9
 
 
 def tile_multiheadattention_pb_l_kernel(tc, values, logw, Wv, Wo, out):
@@ -35,58 +41,59 @@ def tile_multiheadattention_pb_l_kernel(tc, values, logw, Wv, Wo, out):
         make_identity(nc, ident[:])
         warm = keep.tile([P, 8], F32, name="warm")
         nc.scalar.activation(out=warm[:, 0:1], in_=ident[:, 0:1], func=ACT.Copy, scale=1.0)
-        wv_codes = keep.tile([P, 4, DP], U32, name="wv_codes", align_bytes=64)
-        wv_scales = keep.tile([P, 4, DP], U8, name="wv_scales", align_bytes=64)
-        wo_codes = keep.tile([P, 4, DO], U32, name="wo_codes", align_bytes=64)
-        wo_scales = keep.tile([P, 4, DO], U8, name="wo_scales", align_bytes=64)
+
+        wv_codes = keep.tile([P, PASSES, DP], U32, name="wv_codes", align_bytes=64)
+        wv_scales = keep.tile([P, PASSES, DP], U8, name="wv_scales", align_bytes=64)
+        wo_codes = keep.tile([P, PASSES, DO], U32, name="wo_codes", align_bytes=64)
+        wo_scales = keep.tile([P, PASSES, DO], U8, name="wo_scales", align_bytes=64)
 
         jobs = []
-        for bt in range(NB):
+        for bt in range(BATCH_TILES):
             for s in range(SL):
                 jobs.append(("v", s, bt))
                 seen = bt * SL + s + 1
-                if seen % WO_EVERY == 0 and seen // WO_EVERY <= NW:
+                if seen % WO_EVERY == 0 and seen // WO_EVERY <= W_TILES:
                     jobs.append(("wo", seen // WO_EVERY - 1, 0))
-        nj = len(jobs)
-        last_job = [jobs.index(("v", SL - 1, bt)) for bt in range(NB)]
-        s2_first = jobs.index(("wo", NW - 1, 0)) + 2
+        n_jobs = len(jobs)
+        last_job = [jobs.index(("v", SL - 1, bt)) for bt in range(BATCH_TILES)]
+        wo_ready = jobs.index(("wo", W_TILES - 1, 0)) + 2
 
         raw, srt, trn, grp, cod, scl, bank = {}, {}, {}, {}, {}, {}, {}
-        lw, lwb, acc, ga, ac, asc = {}, {}, {}, {}, {}, {}
-        hraw, hsrt, hps, hgrp = {}, {}, {}, {}
+        wv_raw, wv_swapped, wv_grp = {}, {}, {}
+        lw_bf16, lw_f32, acc, total, attn_grp, attn_cod, attn_scl = {}, {}, {}, {}, {}, {}, {}
 
-        def head_load(r):
-            t = stream.tile([P, 4, 512], BF16, name="hraw", tag="hraw", bufs=5)
-            hraw[r] = t
-            nc.sync.dma_start(out=t[:].rearrange("p q k -> p (q k)"), in_=Wv[P * r : P * r + P, :])
-
-        def head_permute(r):
-            t = stream.tile([P, 1024], F32, name="hsrt", tag="hsrt", bufs=2)
-            hsrt[r] = t
-            nc.vector.tensor_copy(
-                out=t[:].rearrange("p (g q w) -> p g q w", g=4, q=4),
-                in_=hraw[r][:].bitcast(F32).rearrange("p q (g w) -> p g q w", g=4),
-            )
-
-        def head_turn(r):
-            gd = stream.tile([P, 2048], BF16, name="hgrp", tag="hgrp", bufs=2, align_bytes=64)
-            hgrp[r] = gd
-            for half in range(2):
-                pt = psum.tile([P, 512], F32, name="mm", tag="mm", bufs=6)
-                for j in range(4):
-                    lo = 256 * (2 * half + j // 2) + j % 2
-                    nc.tensor.transpose(pt[:, P * j : P * j + P], hsrt[r][:, lo : lo + 255 : 2], ident[:])
-                nc.scalar.copy(
-                    out=gd[:].bitcast(F32)[:, 512 * half : 512 * half + 512].rearrange("p (g c u) -> p g c u", g=2, u=2),
-                    in_=pt[:].rearrange("p (g u c) -> p g c u", g=2, u=2),
-                )
-
-        def quantise_weight(gd, codes, scales, block):
-            for g in range(4):
+        def quantise_weight(grouped, codes, scales, block):
+            for g in range(PASSES):
                 nc.vector.quantize_mx(
                     out=codes[:, g, P * block : P * block + P].bitcast(FP8X4),
                     scales=scales[:, g, P * block : P * block + P],
-                    in_=gd[:, 512 * g : 512 * g + 512],
+                    in_=grouped[:, 512 * g : 512 * g + 512],
+                )
+
+        def wv_load(r):
+            t = stream.tile([P, 4, 512], BF16, name="wv_raw", tag="wv_raw", bufs=5)
+            wv_raw[r] = t
+            nc.sync.dma_start(out=t[:].rearrange("p q k -> p (q k)"), in_=Wv[P * r : P * r + P, :])
+
+        def wv_swap(r):
+            t = stream.tile([P, 1024], F32, name="wv_swapped", tag="wv_swapped", bufs=2)
+            wv_swapped[r] = t
+            nc.vector.tensor_copy(
+                out=t[:].rearrange("p (g q w) -> p g q w", g=4, q=4),
+                in_=wv_raw[r][:].bitcast(F32).rearrange("p q (g w) -> p g q w", g=4),
+            )
+
+        def wv_transpose(r):
+            grouped = stream.tile([P, 2048], BF16, name="wv_grp", tag="wv_grp", bufs=3, align_bytes=64)
+            wv_grp[r] = grouped
+            for half in range(2):
+                turned = psum.tile([P, BANK], F32, name="mm", tag="mm", bufs=6)
+                for j in range(4):
+                    first = 256 * (2 * half + j // 2) + j % 2
+                    nc.tensor.transpose(turned[:, P * j : P * j + P], wv_swapped[r][:, first : first + 255 : 2], ident[:])
+                nc.scalar.copy(
+                    out=grouped[:].bitcast(F32)[:, 512 * half : 512 * half + 512].rearrange("p (g c u) -> p g c u", g=2, u=2),
+                    in_=turned[:].rearrange("p (g u c) -> p g c u", g=2, u=2),
                 )
 
         def load(j):
@@ -100,33 +107,29 @@ def tile_multiheadattention_pb_l_kernel(tc, values, logw, Wv, Wo, out):
                     in_=rows[:, 512 * q : 512 * q + 512].rearrange("(tg b) k -> b tg k", b=32),
                 )
             if kind == "v" and a == 0:
-                lwr = stream.tile([P, SL, H], BF16, name="lwr", tag="lwr", bufs=2)
-                nc.sync.dma_start(out=lwr[:], in_=logw[:, P * bt : P * bt + P, :].rearrange("s b h -> b s h"))
-                lwb[bt] = lwr
-                lwf = stream.tile([P, SL, 4, 8], F32, name="lwf", tag="lwf", bufs=2)
-                lw[bt] = lwf
+                lw = stream.tile([P, SL, H], BF16, name="lw_bf16", tag="lw_bf16", bufs=2)
+                lw_bf16[bt] = lw
+                nc.sync.dma_start(out=lw[:], in_=logw[:, P * bt : P * bt + P, :].rearrange("s b h -> b s h"))
 
         def widen_logw(bt):
-            for n in range(4):
-                if POOL_BY[n] == "scalar":
-                    nc.scalar.copy(
-                        out=lw[bt][:, :, n, :].rearrange("p s (a c) -> p s a c", a=4),
-                        in_=lwb[bt][:].rearrange("p s (a m c) -> p s a m c", a=4, m=4)[:, :, :, n, :],
-                    )
+            wide = stream.tile([P, SL, 2, HEADS], F32, name="lw_f32", tag="lw_f32", bufs=2)
+            lw_f32[bt] = wide
+            for n in (0, 2):
+                nc.scalar.copy(
+                    out=wide[:, :, n // 2, :].rearrange("p s (q c) -> p s q c", q=4),
+                    in_=lw_bf16[bt][:].rearrange("p s (q n c) -> p s q n c", q=4, n=4)[:, :, :, n, :],
+                )
 
         def sort(j):
             if jobs[j][0] == "v" and jobs[j][1] == 0:
                 widen_logw(jobs[j][2])
             words = raw[j][:].bitcast(F32)
-            sd = stream.tile([P, 1024], F32, name="srt", tag="srt", bufs=2, align_bytes=64)
-            srt[j] = sd
-            view = sd[:].rearrange("p (g tg u x) -> p g tg u x", g=4, tg=4, u=2)
-            for g in range(4):
-                mover = nc.scalar.copy if g < SORT_ON_SCALAR else nc.vector.tensor_copy
-                mover(
-                    out=view[:, g],
-                    in_=words[:, :, 64 * g : 64 * g + 64].rearrange("p tg (x u) -> p tg u x", u=2),
-                )
+            t = stream.tile([P, 1024], F32, name="srt", tag="srt", bufs=2, align_bytes=64)
+            srt[j] = t
+            blocks = t[:].rearrange("p (g tg u x) -> p g tg u x", g=4, tg=4, u=2)
+            for g in range(PASSES):
+                copy = nc.scalar.copy if g < SORTS_ON_SCALAR else nc.vector.tensor_copy
+                copy(out=blocks[:, g], in_=words[:, :, 64 * g : 64 * g + 64].rearrange("p tg (x u) -> p tg u x", u=2))
 
         def turn(j):
             t = stream.tile([P, 1024], F32, name="trn", tag="trn", bufs=2, align_bytes=64)
@@ -134,10 +137,10 @@ def tile_multiheadattention_pb_l_kernel(tc, values, logw, Wv, Wo, out):
             nc.vector.transpose(out=t[:], in_=srt[j][:])
 
         def interleave(j):
-            gd = stream.tile([P, 2048], BF16, name="grp", tag="grp", bufs=2, align_bytes=64)
-            grp[j] = gd
+            t = stream.tile([P, 2048], BF16, name="grp", tag="grp", bufs=2, align_bytes=64)
+            grp[j] = t
             nc.scalar.copy(
-                out=gd[:].bitcast(F32).rearrange("p (c b u) -> p c b u", c=16, u=2),
+                out=t[:].bitcast(F32).rearrange("p (c b u) -> p c b u", c=16, u=2),
                 in_=trn[j][:].rearrange("p (c u b) -> p c b u", c=16, u=2),
             )
 
@@ -146,8 +149,8 @@ def tile_multiheadattention_pb_l_kernel(tc, values, logw, Wv, Wo, out):
             if kind == "wo":
                 quantise_weight(grp[j], wo_codes, wo_scales, a)
             else:
-                c = stream.tile([P, 512], U32, name="cod", tag="cod", bufs=3, align_bytes=64)
-                sc = stream.tile([P, 512], U8, name="scl", tag="scl", bufs=3, align_bytes=64)
+                c = stream.tile([P, PASSES * P], U32, name="cod", tag="cod", bufs=3, align_bytes=64)
+                sc = stream.tile([P, PASSES * P], U8, name="scl", tag="scl", bufs=3, align_bytes=64)
                 cod[j] = c
                 scl[j] = sc
                 nc.vector.quantize_mx(out=c[:].bitcast(FP8X4), scales=sc[:], in_=grp[j][:])
@@ -157,146 +160,161 @@ def tile_multiheadattention_pb_l_kernel(tc, values, logw, Wv, Wo, out):
                 out=ps[:],
                 lhsT=c[:, P * g : P * g + P].bitcast(FP8X4),
                 lhsT_scale=sc[:, P * g : P * g + P],
-                rhs=w_codes[:, g, 512 * n : 512 * n + 512].bitcast(FP8X4),
-                rhs_scale=w_scales[:, g, 512 * n : 512 * n + 512],
+                rhs=w_codes[:, g, BANK * n : BANK * n + BANK].bitcast(FP8X4),
+                rhs_scale=w_scales[:, g, BANK * n : BANK * n + BANK],
                 start=(g == 0),
-                stop=(g == 3),
+                stop=(g == PASSES - 1),
             )
 
         def mx_group(c, sc, w_codes, w_scales, n):
-            ps = psum.tile([P, 512], F32, name="mm", tag="mm", bufs=6)
-            for g in range(4):
+            ps = psum.tile([P, BANK], F32, name="mm", tag="mm", bufs=6)
+            for g in range(PASSES):
                 mx_pass(ps, c, sc, w_codes, w_scales, n, g)
             return ps
 
-        def pool_bank(j, n):
+        def multiply(j, n):
+            bank[(j, n)] = mx_group(cod[j], scl[j], wv_codes, wv_scales, n)
+
+        def sum_tiles(j, n):
             s, bt = jobs[j][1], jobs[j][2]
-            ps = bank[(j, n)]
             if s == 0:
-                a_new = stream.tile([P, 512], F32, name="acc%d" % n, tag="acc%d" % n, bufs=2)
-                acc[(bt, n)] = a_new
-            a = acc[(bt, n)]
-            w = lw[bt][:, s, n, :]
-            how = POOL_BY[n]
-            if how == "vector":
-                for hh in range(8):
-                    cols = slice(64 * hh, 64 * hh + 64)
-                    h = 8 * (hh // 2) + 2 * n + hh % 2
-                    wb = lwb[bt][:, s, h : h + 1]
-                    if s == 0:
-                        nc.vector.tensor_scalar(out=a[:, cols], in0=ps[:, cols], scalar1=wb, scalar2=None, op0=ALU.mult)
-                    else:
-                        nc.vector.scalar_tensor_tensor(out=a[:, cols], in0=ps[:, cols], scalar=wb, in1=a[:, cols], op0=ALU.mult, op1=ALU.add)
-                return
-            if s == 0:
-                dst = a
-            else:
-                dst = stream.tile([P, 512], F32, name="tmp", tag="tmp", bufs=4)
-            if how == "scalar":
-                for hh in range(8):
-                    cols = slice(64 * hh, 64 * hh + 64)
-                    nc.scalar.activation(out=dst[:, cols], in_=ps[:, cols], func=ACT.Copy, scale=w[:, hh : hh + 1])
-            else:
-                nc.vector.tensor_tensor(
-                    out=dst[:].rearrange("p (h c) -> p h c", h=8),
-                    in0=ps[:].rearrange("p (h c) -> p h c", h=8),
-                    in1=w.rearrange("p (h o) -> p h o", o=1).to_broadcast([P, 8, 64]),
-                    op=ALU.mult,
-                )
-            if s > 0:
-                for part in range(2):
-                    cs = slice(256 * part, 256 * part + 256)
-                    nc.gpsimd.tensor_tensor(out=a[:, cs], in0=a[:, cs], in1=dst[:, cs], op=ALU.add)
+                a = stream.tile([P, BANK], F32, name="acc%d" % n, tag="acc%d" % n, bufs=2)
+                acc[(bt, n)] = a
+            if s == SL - 1:
+                f = stream.tile([P, 4, P], F32, name="total%d" % n, tag="total%d" % n, bufs=1)
+                total[(bt, n)] = f
+            return s, bt, bank[(j, n)], acc[(bt, n)]
 
-        def s2_turn(bt, g):
-            if bt not in ga:
-                g_new = stream.tile([P, 2048], BF16, name="ga", tag="ga", bufs=2, align_bytes=64)
-                ga[bt] = g_new
-                c = stream.tile([P, 512], U32, name="ac", tag="ac", bufs=4, align_bytes=64)
-                sc = stream.tile([P, 512], U8, name="asc", tag="asc", bufs=4, align_bytes=64)
-                ac[bt] = c
-                asc[bt] = sc
-            tp = psum.tile([P, 4, P], F32, name="tp", tag="tp", bufs=2)
+        def pool_on_vector(j, n):
+            s, bt, ps, a = sum_tiles(j, n)
+            for hh in range(HEADS):
+                cols = slice(NH * hh, NH * hh + NH)
+                h = 8 * (hh // 2) + 2 * n + hh % 2
+                w = lw_bf16[bt][:, s, h : h + 1]
+                if s == 0:
+                    nc.vector.tensor_scalar(out=a[:, cols], in0=ps[:, cols], scalar1=w, scalar2=None, op0=ALU.mult)
+                elif s < SL - 1:
+                    nc.vector.scalar_tensor_tensor(out=a[:, cols], in0=ps[:, cols], scalar=w, in1=a[:, cols], op0=ALU.mult, op1=ALU.add)
+                else:
+                    nc.vector.scalar_tensor_tensor(
+                        out=total[(bt, n)][:, :, 16 * hh : 16 * hh + 16],
+                        in0=ps[:, cols].rearrange("p (x t) -> p t x", t=4),
+                        scalar=w,
+                        in1=a[:, cols].rearrange("p (x t) -> p t x", t=4),
+                        op0=ALU.mult,
+                        op1=ALU.add,
+                    )
+
+        def pool_on_scalar(j, n):
+            s, bt, ps, a = sum_tiles(j, n)
+            scaled = a if s == 0 else stream.tile([P, BANK], F32, name="scaled", tag="scaled", bufs=3)
+            for hh in range(HEADS):
+                cols = slice(NH * hh, NH * hh + NH)
+                nc.scalar.activation(out=scaled[:, cols], in_=ps[:, cols], func=ACT.Copy, scale=lw_f32[bt][:, s, n // 2, hh : hh + 1])
+            for half in range(2):
+                if 0 < s < SL - 1:
+                    cols = slice(256 * half, 256 * half + 256)
+                    nc.gpsimd.tensor_tensor(out=a[:, cols], in0=a[:, cols], in1=scaled[:, cols], op=ALU.add)
+                elif s == SL - 1:
+                    ts = slice(2 * half, 2 * half + 2)
+                    nc.gpsimd.tensor_tensor(
+                        out=total[(bt, n)][:, ts, :],
+                        in0=a[:].rearrange("p (x t) -> p t x", t=4)[:, ts, :],
+                        in1=scaled[:].rearrange("p (x t) -> p t x", t=4)[:, ts, :],
+                        op=ALU.add,
+                    )
+
+        def attn_transpose(bt, g):
+            if g == 0:
+                grouped = stream.tile([P, 2048], BF16, name="attn_grp", tag="attn_grp", bufs=1, align_bytes=64)
+                c = stream.tile([P, PASSES * P], U32, name="attn_cod", tag="attn_cod", bufs=4, align_bytes=64)
+                sc = stream.tile([P, PASSES * P], U8, name="attn_scl", tag="attn_scl", bufs=4, align_bytes=64)
+                attn_grp[bt], attn_cod[bt], attn_scl[bt] = grouped, c, sc
+            turned = psum.tile([P, 4, P], F32, name="tp", tag="tp", bufs=2)
             for t in range(4):
-                nc.tensor.transpose(tp[:, t, :], acc[(bt, g)][:, t : t + 509 : 4], ident[:])
+                nc.tensor.transpose(turned[:, t, :], total[(bt, g)][:, t, :], ident[:])
             nc.scalar.copy(
-                out=ga[bt][:, 512 * g : 512 * g + 512].rearrange("p (b t) -> p b t", t=4),
-                in_=tp[:].rearrange("p t b -> p b t"),
+                out=attn_grp[bt][:, 512 * g : 512 * g + 512].rearrange("p (b t) -> p b t", t=4),
+                in_=turned[:].rearrange("p t b -> p b t"),
             )
 
-        def s2_quantise(bt, g):
+        def attn_quantise(bt, g):
             nc.vector.quantize_mx(
-                out=ac[bt][:, P * g : P * g + P].bitcast(FP8X4),
-                scales=asc[bt][:, P * g : P * g + P],
-                in_=ga[bt][:, 512 * g : 512 * g + 512],
+                out=attn_cod[bt][:, P * g : P * g + P].bitcast(FP8X4),
+                scales=attn_scl[bt][:, P * g : P * g + P],
+                in_=attn_grp[bt][:, 512 * g : 512 * g + 512],
             )
 
-        def s2_store(bt, n, ps, engine, queue):
-            ob = stream.tile([P, 512], F32, name="ob", tag="ob", bufs=4)
-            if engine == "scalar":
-                nc.scalar.copy(out=ob[:], in_=ps[:])
-            else:
-                nc.vector.tensor_copy(out=ob[:], in_=ps[:])
-            queue.dma_start(out=out[P * bt : P * bt + P, 512 * n : 512 * n + 512], in_=ob[:])
+        def store(bt, n, ps, copy, queue):
+            result = stream.tile([P, BANK], F32, name="result", tag="result", bufs=4)
+            copy(out=result[:], in_=ps[:])
+            queue.dma_start(out=out[P * bt : P * bt + P, BANK * n : BANK * n + BANK], in_=result[:])
 
-        def step_body(step):
-            for bt in range(NB - 1):
-                late = step - last_job[bt]
+        def step(i):
+            def due(ahead):
+                return 0 <= i + ahead < n_jobs
+
+            for bt in range(BATCH_TILES - 1):
+                late = i - last_job[bt]
                 if late == 2 or late == 3:
-                    s2_turn(bt, 2 * late - 4)
-                    s2_turn(bt, 2 * late - 3)
+                    attn_transpose(bt, 2 * late - 4)
+                    attn_transpose(bt, 2 * late - 3)
                 if late == 4:
-                    for g in range(4):
-                        s2_quantise(bt, g)
-            if 0 <= step - s2_first < 4 * (NB - 1):
-                bt, n = divmod(step - s2_first, 4)
-                s2_store(bt, n, mx_group(ac[bt], asc[bt], wo_codes, wo_scales, n), "scalar", nc.gpsimd)
-            if 0 <= step + 6 < nj:
-                load(step + 6)
-            if 0 <= step + 2 < nj:
-                interleave(step + 2)
-            if 0 <= step + 1 < nj:
-                quantise(step + 1)
-            for j in (step - 2, step - 1):
-                if (j, 3) in bank and (j, 3) not in pooled:
-                    pool_bank(j, 3)
-                    pooled.add((j, 3))
-            if 0 <= step + 3 < nj:
-                turn(step + 3)
-            live = 0 <= step < nj and jobs[step][0] == "v"
-            if live:
-                bank[(step, 0)] = mx_group(cod[step], scl[step], wv_codes, wv_scales, 0)
-                pool_bank(step, 0)
-            if 0 <= step + 4 < nj:
-                sort(step + 4)
-            if live:
-                for n in (1, 2):
-                    bank[(step, n)] = mx_group(cod[step], scl[step], wv_codes, wv_scales, n)
-                    pool_bank(step, n)
-                bank[(step, 3)] = mx_group(cod[step], scl[step], wv_codes, wv_scales, 3)
+                    for g in range(PASSES):
+                        attn_quantise(bt, g)
+            if 0 <= i - wo_ready < BANKS * (BATCH_TILES - 1):
+                bt, n = divmod(i - wo_ready, BANKS)
+                store(bt, n, mx_group(attn_cod[bt], attn_scl[bt], wo_codes, wo_scales, n), nc.scalar.copy, nc.gpsimd)
+            if due(LOAD_AHEAD):
+                load(i + LOAD_AHEAD)
+            if due(INTERLEAVE_AHEAD):
+                interleave(i + INTERLEAVE_AHEAD)
+            if due(QUANTISE_AHEAD):
+                quantise(i + QUANTISE_AHEAD)
+            for j in (i - 2, i - 1):
+                if (j, 3) in bank and (j, 3) not in emptied:
+                    pool_on_vector(j, 3)
+                    emptied.add((j, 3))
+            if due(TURN_AHEAD):
+                turn(i + TURN_AHEAD)
+            token_tile = due(0) and jobs[i][0] == "v"
+            if token_tile:
+                multiply(i, 0)
+                pool_on_scalar(i, 0)
+            if due(SORT_AHEAD):
+                sort(i + SORT_AHEAD)
+            if token_tile:
+                multiply(i, 1)
+                pool_on_vector(i, 1)
+                multiply(i, 2)
+                pool_on_scalar(i, 2)
+                multiply(i, 3)
 
-        pooled = set()
-        for r in range(-4, NW + 1):
-            if 0 <= r < NW:
-                quantise_weight(hgrp[r], wv_codes, wv_scales, 4 * (r % 4) + r // 4)
-            if 0 <= r + 1 < NW:
-                head_turn(r + 1)
-            if 0 <= r + 2 < NW:
-                head_permute(r + 2)
-            if r + 4 < NW:
-                head_load(r + 4)
-            if 4 <= r < NW and r % 2 == 0:
-                step_body((r - 4) // 2 - 6)
-        for step in range(0, nj + 2):
-            step_body(step)
+        emptied = set()
+        for r in range(-4, W_TILES + 1):
+            if 0 <= r - 1:
+                quantise_weight(wv_grp[r - 1], wv_codes, wv_scales, 4 * ((r - 1) % 4) + (r - 1) // 4)
+            if 0 <= r + 1 < W_TILES:
+                wv_transpose(r + 1)
+            if 0 <= r + 2 < W_TILES:
+                wv_swap(r + 2)
+            if r + 4 < W_TILES:
+                wv_load(r + 4)
+            if STREAM_STARTS <= r < STREAM_STARTS + LOAD_AHEAD:
+                step(r - STREAM_STARTS - LOAD_AHEAD)
+        for i in range(n_jobs + 2):
+            step(i)
 
-        bt = NB - 1
-        for g in range(4):
-            s2_turn(bt, g)
-            s2_quantise(bt, g)
-        ends = [psum.tile([P, 512], F32, name="mm", tag="mm", bufs=6) for n in range(4)]
-        for g in range(4):
-            for n in range(4):
-                mx_pass(ends[n], ac[bt], asc[bt], wo_codes, wo_scales, n, g)
-        for n in range(4):
-            s2_store(bt, n, ends[n], "scalar" if n % 2 == 0 else "vector", nc.sync if n % 2 == 0 else nc.scalar)
+        bt = BATCH_TILES - 1
+        for g in range(PASSES):
+            attn_transpose(bt, g)
+            attn_quantise(bt, g)
+        ends = [psum.tile([P, BANK], F32, name="mm", tag="mm", bufs=6) for n in range(BANKS)]
+        for g in range(PASSES):
+            for n in range(BANKS):
+                mx_pass(ends[n], attn_cod[bt], attn_scl[bt], wo_codes, wo_scales, n, g)
+        for n in range(BANKS):
+            if n % 2 == 0:
+                store(bt, n, ends[n], nc.scalar.copy, nc.scalar)
+            else:
+                store(bt, n, ends[n], nc.vector.tensor_copy, nc.sync)

@@ -27,6 +27,7 @@ WO_EVERY = 6
 SORTS_ON_SCALAR = 3
 LOAD_AHEAD, SORT_AHEAD, TURN_AHEAD, INTERLEAVE_AHEAD, QUANTISE_AHEAD = 6, 4, 3, 2, 1
 STREAM_STARTS = 9
+MX_ALIGN = 256
 
 
 def tile_multiheadattention_pb_l_kernel(tc, values, logw, Wv, Wo, out):
@@ -42,10 +43,10 @@ def tile_multiheadattention_pb_l_kernel(tc, values, logw, Wv, Wo, out):
         warm = keep.tile([P, 8], F32, name="warm")
         nc.scalar.activation(out=warm[:, 0:1], in_=ident[:, 0:1], func=ACT.Copy, scale=1.0)
 
-        wv_codes = keep.tile([P, PASSES, DP], U32, name="wv_codes", align_bytes=64)
-        wv_scales = keep.tile([P, PASSES, DP], U8, name="wv_scales", align_bytes=64)
-        wo_codes = keep.tile([P, PASSES, DO], U32, name="wo_codes", align_bytes=64)
-        wo_scales = keep.tile([P, PASSES, DO], U8, name="wo_scales", align_bytes=64)
+        wv_codes = keep.tile([P, PASSES, DP], U32, name="wv_codes", align_bytes=MX_ALIGN)
+        wv_scales = keep.tile([P, PASSES, DP], U8, name="wv_scales", align_bytes=MX_ALIGN)
+        wo_codes = keep.tile([P, PASSES, DO], U32, name="wo_codes", align_bytes=MX_ALIGN)
+        wo_scales = keep.tile([P, PASSES, DO], U8, name="wo_scales", align_bytes=MX_ALIGN)
 
         jobs = []
         for bt in range(BATCH_TILES):
@@ -149,8 +150,8 @@ def tile_multiheadattention_pb_l_kernel(tc, values, logw, Wv, Wo, out):
             if kind == "wo":
                 quantise_weight(grp[j], wo_codes, wo_scales, a)
             else:
-                c = stream.tile([P, PASSES * P], U32, name="cod", tag="cod", bufs=3, align_bytes=64)
-                sc = stream.tile([P, PASSES * P], U8, name="scl", tag="scl", bufs=3, align_bytes=64)
+                c = stream.tile([P, PASSES * P], U32, name="cod", tag="cod", bufs=3, align_bytes=MX_ALIGN)
+                sc = stream.tile([P, PASSES * P], U8, name="scl", tag="scl", bufs=3, align_bytes=MX_ALIGN)
                 cod[j] = c
                 scl[j] = sc
                 nc.vector.quantize_mx(out=c[:].bitcast(FP8X4), scales=sc[:], in_=grp[j][:])
@@ -227,8 +228,8 @@ def tile_multiheadattention_pb_l_kernel(tc, values, logw, Wv, Wo, out):
         def attn_transpose(bt, g):
             if g == 0:
                 grouped = stream.tile([P, 2048], BF16, name="attn_grp", tag="attn_grp", bufs=1, align_bytes=64)
-                c = stream.tile([P, PASSES * P], U32, name="attn_cod", tag="attn_cod", bufs=4, align_bytes=64)
-                sc = stream.tile([P, PASSES * P], U8, name="attn_scl", tag="attn_scl", bufs=4, align_bytes=64)
+                c = stream.tile([P, PASSES * P], U32, name="attn_cod", tag="attn_cod", bufs=4, align_bytes=MX_ALIGN)
+                sc = stream.tile([P, PASSES * P], U8, name="attn_scl", tag="attn_scl", bufs=4, align_bytes=MX_ALIGN)
                 attn_grp[bt], attn_cod[bt], attn_scl[bt] = grouped, c, sc
             turned = psum.tile([P, 4, P], F32, name="tp", tag="tp", bufs=2)
             for t in range(4):

from contextlib import ExitStack

import concourse.mybir as mybir
from concourse.masks import make_identity

SL, BS, DM, H, NH, DO = 32, 512, 2048, 32, 64, 2048
DP = H * NH
FLOPS = 2 * SL * BS * DM * DP + 2 * BS * DP * DO

F32 = mybir.dt.float32
BF16 = mybir.dt.bfloat16
U32 = mybir.dt.uint32
U8 = mybir.dt.uint8
FP8X4 = mybir.dt.float8_e4m3fn_x4
ALU = mybir.AluOpType
ACT = mybir.ActivationFunctionType

P = 128
PASSES = 4
BANK = 512
BANKS = DP // BANK
HEADS = BANK // NH
BATCH_TILES = BS // P
W_TILES = DP // P

WO_EVERY = 6
SORTS_ON_SCALAR = 3
LOAD_AHEAD, SORT_AHEAD, TURN_AHEAD, INTERLEAVE_AHEAD, QUANTISE_AHEAD = 6, 4, 3, 2, 1
STREAM_STARTS = 9
MX_ALIGN = 256


def tile_multiheadattention_pb_l_kernel(tc, values, logw, Wv, Wo, out):
    nc = tc.nc
    with ExitStack() as ctx:
        keep = ctx.enter_context(tc.tile_pool(name="keep", bufs=1))
        stream = ctx.enter_context(tc.tile_pool(name="stream", bufs=2))
        psum = ctx.enter_context(tc.psum_pool(name="psum", bufs=2))
        ctx.enter_context(tc.manual_schedule())

        ident = keep.tile([P, P], F32, name="ident")
        make_identity(nc, ident[:])
        warm = keep.tile([P, 8], F32, name="warm")
        nc.scalar.activation(out=warm[:, 0:1], in_=ident[:, 0:1], func=ACT.Copy, scale=1.0)

        wv_codes = keep.tile([P, PASSES, DP], U32, name="wv_codes", align_bytes=MX_ALIGN)
        wv_scales = keep.tile([P, PASSES, DP], U8, name="wv_scales", align_bytes=MX_ALIGN)
        wo_codes = keep.tile([P, PASSES, DO], U32, name="wo_codes", align_bytes=MX_ALIGN)
        wo_scales = keep.tile([P, PASSES, DO], U8, name="wo_scales", align_bytes=MX_ALIGN)

        jobs = []
        for bt in range(BATCH_TILES):
            for s in range(SL):
                jobs.append(("v", s, bt))
                seen = bt * SL + s + 1
                if seen % WO_EVERY == 0 and seen // WO_EVERY <= W_TILES:
                    jobs.append(("wo", seen // WO_EVERY - 1, 0))
        n_jobs = len(jobs)
        last_job = [jobs.index(("v", SL - 1, bt)) for bt in range(BATCH_TILES)]
        wo_ready = jobs.index(("wo", W_TILES - 1, 0)) + 2

        raw, srt, trn, grp, cod, scl, bank = {}, {}, {}, {}, {}, {}, {}
        wv_raw, wv_swapped, wv_grp = {}, {}, {}
        lw_bf16, lw_f32, acc, total, attn_grp, attn_cod, attn_scl = {}, {}, {}, {}, {}, {}, {}

        def quantise_weight(grouped, codes, scales, block):
            for g in range(PASSES):
                nc.vector.quantize_mx(
                    out=codes[:, g, P * block : P * block + P].bitcast(FP8X4),
                    scales=scales[:, g, P * block : P * block + P],
                    in_=grouped[:, 512 * g : 512 * g + 512],
                )

        def wv_load(r):
            t = stream.tile([P, 4, 512], BF16, name="wv_raw", tag="wv_raw", bufs=5)
            wv_raw[r] = t
            nc.sync.dma_start(out=t[:].rearrange("p q k -> p (q k)"), in_=Wv[P * r : P * r + P, :])

        def wv_swap(r):
            t = stream.tile([P, 1024], F32, name="wv_swapped", tag="wv_swapped", bufs=2)
            wv_swapped[r] = t
            nc.vector.tensor_copy(
                out=t[:].rearrange("p (g q w) -> p g q w", g=4, q=4),
                in_=wv_raw[r][:].bitcast(F32).rearrange("p q (g w) -> p g q w", g=4),
            )

        def wv_transpose(r):
            grouped = stream.tile([P, 2048], BF16, name="wv_grp", tag="wv_grp", bufs=3, align_bytes=64)
            wv_grp[r] = grouped
            for half in range(2):
                turned = psum.tile([P, BANK], F32, name="mm", tag="mm", bufs=6)
                for j in range(4):
                    first = 256 * (2 * half + j // 2) + j % 2
                    nc.tensor.transpose(turned[:, P * j : P * j + P], wv_swapped[r][:, first : first + 255 : 2], ident[:])
                nc.scalar.copy(
                    out=grouped[:].bitcast(F32)[:, 512 * half : 512 * half + 512].rearrange("p (g c u) -> p g c u", g=2, u=2),
                    in_=turned[:].rearrange("p (g u c) -> p g c u", g=2, u=2),
                )

        def load(j):
            kind, a, bt = jobs[j]
            rows = Wo[P * a : P * a + P, :] if kind == "wo" else values[a, P * bt : P * bt + P, :]
            r = stream.tile([P, 4, 512], BF16, name="raw", tag="raw", bufs=4)
            raw[j] = r
            for q in range(4):
                nc.sync.dma_start(
                    out=r[32 * q : 32 * q + 32, :, :],
                    in_=rows[:, 512 * q : 512 * q + 512].rearrange("(tg b) k -> b tg k", b=32),
                )
            if kind == "v" and a == 0:
                lw = stream.tile([P, SL, H], BF16, name="lw_bf16", tag="lw_bf16", bufs=2)
                lw_bf16[bt] = lw
                nc.sync.dma_start(out=lw[:], in_=logw[:, P * bt : P * bt + P, :].rearrange("s b h -> b s h"))

        def widen_logw(bt):
            wide = stream.tile([P, SL, 2, HEADS], F32, name="lw_f32", tag="lw_f32", bufs=2)
            lw_f32[bt] = wide
            for n in (0, 2):
                nc.scalar.copy(
                    out=wide[:, :, n // 2, :].rearrange("p s (q c) -> p s q c", q=4),
                    in_=lw_bf16[bt][:].rearrange("p s (q n c) -> p s q n c", q=4, n=4)[:, :, :, n, :],
                )

        def sort(j):
            if jobs[j][0] == "v" and jobs[j][1] == 0:
                widen_logw(jobs[j][2])
            words = raw[j][:].bitcast(F32)
            t = stream.tile([P, 1024], F32, name="srt", tag="srt", bufs=2, align_bytes=64)
            srt[j] = t
            blocks = t[:].rearrange("p (g tg u x) -> p g tg u x", g=4, tg=4, u=2)
            for g in range(PASSES):
                copy = nc.scalar.copy if g < SORTS_ON_SCALAR else nc.vector.tensor_copy
                copy(out=blocks[:, g], in_=words[:, :, 64 * g : 64 * g + 64].rearrange("p tg (x u) -> p tg u x", u=2))

        def turn(j):
            t = stream.tile([P, 1024], F32, name="trn", tag="trn", bufs=2, align_bytes=64)
            trn[j] = t
            nc.vector.transpose(out=t[:], in_=srt[j][:])

        def interleave(j):
            t = stream.tile([P, 2048], BF16, name="grp", tag="grp", bufs=2, align_bytes=64)
            grp[j] = t
            nc.scalar.copy(
                out=t[:].bitcast(F32).rearrange("p (c b u) -> p c b u", c=16, u=2),
                in_=trn[j][:].rearrange("p (c u b) -> p c b u", c=16, u=2),
            )

        def quantise(j):
            kind, a, bt = jobs[j]
            if kind == "wo":
                quantise_weight(grp[j], wo_codes, wo_scales, a)
            else:
                c = stream.tile([P, PASSES * P], U32, name="cod", tag="cod", bufs=3, align_bytes=MX_ALIGN)
                sc = stream.tile([P, PASSES * P], U8, name="scl", tag="scl", bufs=3, align_bytes=MX_ALIGN)
                cod[j] = c
                scl[j] = sc
                nc.vector.quantize_mx(out=c[:].bitcast(FP8X4), scales=sc[:], in_=grp[j][:])

        def mx_pass(ps, c, sc, w_codes, w_scales, n, g):
            nc.tensor.matmul_mx(
                out=ps[:],
                lhsT=c[:, P * g : P * g + P].bitcast(FP8X4),
                lhsT_scale=sc[:, P * g : P * g + P],
                rhs=w_codes[:, g, BANK * n : BANK * n + BANK].bitcast(FP8X4),
                rhs_scale=w_scales[:, g, BANK * n : BANK * n + BANK],
                start=(g == 0),
                stop=(g == PASSES - 1),
            )

        def mx_group(c, sc, w_codes, w_scales, n):
            ps = psum.tile([P, BANK], F32, name="mm", tag="mm", bufs=6)
            for g in range(PASSES):
                mx_pass(ps, c, sc, w_codes, w_scales, n, g)
            return ps

        def multiply(j, n):
            bank[(j, n)] = mx_group(cod[j], scl[j], wv_codes, wv_scales, n)

        def sum_tiles(j, n):
            s, bt = jobs[j][1], jobs[j][2]
            if s == 0:
                a = stream.tile([P, BANK], F32, name="acc%d" % n, tag="acc%d" % n, bufs=2)
                acc[(bt, n)] = a
            if s == SL - 1:
                f = stream.tile([P, 4, P], F32, name="total%d" % n, tag="total%d" % n, bufs=1)
                total[(bt, n)] = f
            return s, bt, bank[(j, n)], acc[(bt, n)]

        def pool_on_vector(j, n):
            s, bt, ps, a = sum_tiles(j, n)
            for hh in range(HEADS):
                cols = slice(NH * hh, NH * hh + NH)
                h = 8 * (hh // 2) + 2 * n + hh % 2
                w = lw_bf16[bt][:, s, h : h + 1]
                if s == 0:
                    nc.vector.tensor_scalar(out=a[:, cols], in0=ps[:, cols], scalar1=w, scalar2=None, op0=ALU.mult)
                elif s < SL - 1:
                    nc.vector.scalar_tensor_tensor(out=a[:, cols], in0=ps[:, cols], scalar=w, in1=a[:, cols], op0=ALU.mult, op1=ALU.add)
                else:
                    nc.vector.scalar_tensor_tensor(
                        out=total[(bt, n)][:, :, 16 * hh : 16 * hh + 16],
                        in0=ps[:, cols].rearrange("p (x t) -> p t x", t=4),
                        scalar=w,
                        in1=a[:, cols].rearrange("p (x t) -> p t x", t=4),
                        op0=ALU.mult,
                        op1=ALU.add,
                    )

        def pool_on_scalar(j, n):
            s, bt, ps, a = sum_tiles(j, n)
            scaled = a if s == 0 else stream.tile([P, BANK], F32, name="scaled", tag="scaled", bufs=3)
            for hh in range(HEADS):
                cols = slice(NH * hh, NH * hh + NH)
                nc.scalar.activation(out=scaled[:, cols], in_=ps[:, cols], func=ACT.Copy, scale=lw_f32[bt][:, s, n // 2, hh : hh + 1])
            for half in range(2):
                if 0 < s < SL - 1:
                    cols = slice(256 * half, 256 * half + 256)
                    nc.gpsimd.tensor_tensor(out=a[:, cols], in0=a[:, cols], in1=scaled[:, cols], op=ALU.add)
                elif s == SL - 1:
                    ts = slice(2 * half, 2 * half + 2)
                    nc.gpsimd.tensor_tensor(
                        out=total[(bt, n)][:, ts, :],
                        in0=a[:].rearrange("p (x t) -> p t x", t=4)[:, ts, :],
                        in1=scaled[:].rearrange("p (x t) -> p t x", t=4)[:, ts, :],
                        op=ALU.add,
                    )

        def attn_transpose(bt, g):
            if g == 0:
                grouped = stream.tile([P, 2048], BF16, name="attn_grp", tag="attn_grp", bufs=1, align_bytes=64)
                c = stream.tile([P, PASSES * P], U32, name="attn_cod", tag="attn_cod", bufs=4, align_bytes=MX_ALIGN)
                sc = stream.tile([P, PASSES * P], U8, name="attn_scl", tag="attn_scl", bufs=4, align_bytes=MX_ALIGN)
                attn_grp[bt], attn_cod[bt], attn_scl[bt] = grouped, c, sc
            turned = psum.tile([P, 4, P], F32, name="tp", tag="tp", bufs=2)
            for t in range(4):
                nc.tensor.transpose(turned[:, t, :], total[(bt, g)][:, t, :], ident[:])
            nc.scalar.copy(
                out=attn_grp[bt][:, 512 * g : 512 * g + 512].rearrange("p (b t) -> p b t", t=4),
                in_=turned[:].rearrange("p t b -> p b t"),
            )

        def attn_quantise(bt, g):
            nc.vector.quantize_mx(
                out=attn_cod[bt][:, P * g : P * g + P].bitcast(FP8X4),
                scales=attn_scl[bt][:, P * g : P * g + P],
                in_=attn_grp[bt][:, 512 * g : 512 * g + 512],
            )

        def store(bt, n, ps, copy, queue):
            result = stream.tile([P, BANK], F32, name="result", tag="result", bufs=4)
            copy(out=result[:], in_=ps[:])
            queue.dma_start(out=out[P * bt : P * bt + P, BANK * n : BANK * n + BANK], in_=result[:])

        def step(i):
            def due(ahead):
                return 0 <= i + ahead < n_jobs

            for bt in range(BATCH_TILES - 1):
                late = i - last_job[bt]
                if late == 2 or late == 3:
                    attn_transpose(bt, 2 * late - 4)
                    attn_transpose(bt, 2 * late - 3)
                if late == 4:
                    for g in range(PASSES):
                        attn_quantise(bt, g)
            if 0 <= i - wo_ready < BANKS * (BATCH_TILES - 1):
                bt, n = divmod(i - wo_ready, BANKS)
                store(bt, n, mx_group(attn_cod[bt], attn_scl[bt], wo_codes, wo_scales, n), nc.scalar.copy, nc.gpsimd)
            if due(LOAD_AHEAD):
                load(i + LOAD_AHEAD)
            if due(INTERLEAVE_AHEAD):
                interleave(i + INTERLEAVE_AHEAD)
            if due(QUANTISE_AHEAD):
                quantise(i + QUANTISE_AHEAD)
            for j in (i - 2, i - 1):
                if (j, 3) in bank and (j, 3) not in emptied:
                    pool_on_vector(j, 3)
                    emptied.add((j, 3))
            if due(TURN_AHEAD):
                turn(i + TURN_AHEAD)
            token_tile = due(0) and jobs[i][0] == "v"
            if token_tile:
                multiply(i, 0)
                pool_on_scalar(i, 0)
            if due(SORT_AHEAD):
                sort(i + SORT_AHEAD)
            if token_tile:
                multiply(i, 1)
                pool_on_vector(i, 1)
                multiply(i, 2)
                pool_on_scalar(i, 2)
                multiply(i, 3)

        emptied = set()
        for r in range(-4, W_TILES + 1):
            if 0 <= r - 1:
                quantise_weight(wv_grp[r - 1], wv_codes, wv_scales, 4 * ((r - 1) % 4) + (r - 1) // 4)
            if 0 <= r + 1 < W_TILES:
                wv_transpose(r + 1)
            if 0 <= r + 2 < W_TILES:
                wv_swap(r + 2)
            if r + 4 < W_TILES:
                wv_load(r + 4)
            if STREAM_STARTS <= r < STREAM_STARTS + LOAD_AHEAD:
                step(r - STREAM_STARTS - LOAD_AHEAD)
        for i in range(n_jobs + 2):
            step(i)

        bt = BATCH_TILES - 1
        for g in range(PASSES):
            attn_transpose(bt, g)
            attn_quantise(bt, g)
        ends = [psum.tile([P, BANK], F32, name="mm", tag="mm", bufs=6) for n in range(BANKS)]
        for g in range(PASSES):
            for n in range(BANKS):
                mx_pass(ends[n], attn_cod[bt], attn_scl[bt], wo_codes, wo_scales, n, g)
        for n in range(BANKS):
            if n % 2 == 0:
                store(bt, n, ends[n], nc.scalar.copy, nc.scalar)
            else:
                store(bt, n, ends[n], nc.vector.tensor_copy, nc.sync)
